import numpy as np
import ml_dtypes


def mxq(x, axis, fmt="e4m3"):
    dtype, down = {"e4m3": (ml_dtypes.float8_e4m3fn, 7), "e5m2": (ml_dtypes.float8_e5m2, 14)}[fmt]
    v = np.moveaxis(np.asarray(x, np.float32).astype(ml_dtypes.bfloat16).astype(np.float64), axis, -1)
    blocks = v.reshape(v.shape[:-1] + (-1, 32))
    amax = np.abs(blocks).max(-1, keepdims=True)
    byte = np.maximum(np.where(amax > 0, np.frexp(amax)[1] - 1 + 127, 0) - down, 1)
    scale = np.exp2(byte - 127.0)
    codes = (blocks / scale).astype(np.float32).astype(dtype).astype(np.float64)
    return np.moveaxis((codes * scale).reshape(v.shape), -1, axis)


WIDE = False


def mx_kscale(k):
    if not WIDE:
        return np.ones(k)
    levels = np.array([10, -10, 5, -5, 0])
    a = np.random.permutation(np.resize(levels, k // 512 * 4)).reshape(k // 512, 4)
    idx = np.arange(k)
    return np.exp2(a[idx // 512, idx % 128 // 32])


BF16 = ml_dtypes.bfloat16


def bf(x):
    return np.asarray(x, np.float32).astype(BF16)


def f64(x):
    return np.asarray(x).astype(np.float64)


N, B, T = 512, 16, 512


def setup_inputs():
    s = mx_kscale(T)
    p = np.random.random(N)
    p = np.where(p < 0.05, 0.0, p)
    edge = np.random.random((N, N)) < p[None, :]
    return {"x": bf(np.random.standard_normal((B, T, N)) * 2.0 * s[None, :, None]),
            "edge_w": bf(edge * 0.4 * N * (0.5 + np.random.random((N, N)))),
            "weight": bf(np.random.standard_normal((T, T)) * 3.0 / np.sqrt(T) / s[:, None]),
            "bias": bf(np.random.standard_normal(T) * 0.1)}


def reference(x, edge_w, weight, bias):
    xp = f64(x).transpose(2, 0, 1)
    W = f64(edge_w)
    deg = W.sum(axis=0)
    dinv = np.where(deg > 0, np.where(deg > 0, deg, 1.0) ** -0.5, 0.0)
    Wn = dinv[:, None] * W * dinv[None, :]
    xw = mxq(xp, 2, "e4m3") @ mxq(f64(weight), 0, "e4m3")
    out = (mxq(Wn, 0, "e4m3").T @ mxq(xw.reshape(N, B * T), 0, "e4m3")).reshape(N, B, T) + f64(bias)
    return out.transpose(1, 2, 0)

@@ -1,0 +1,229 @@
+from contextlib import ExitStack
+
+import concourse.mybir as mybir
+from concourse.masks import make_identity
+
+F32 = mybir.dt.float32
+BF16 = mybir.dt.bfloat16
+U32 = mybir.dt.uint32
+U8 = mybir.dt.uint8
+FP8X4 = mybir.dt.float8_e4m3fn_x4
+ALU = mybir.AluOpType
+ACT = mybir.ActivationFunctionType
+
+P = 128
+PACK = 4
+NODES = 512
+BATCH = 16
+TIME = 512
+FLOPS = 2 * 2 * NODES * BATCH * TIME * TIME
+
+PIN = True
+
+
+def tile_graphembedding_pa_t_kernel(tc, x, edge_w, weight, bias, out):
+    nc = tc.nc
+    with ExitStack() as ctx:
+        if PIN:
+            ctx.enter_context(tc.manual_schedule())
+        const = ctx.enter_context(tc.tile_pool(name="const", bufs=1))
+        xraw_pool = ctx.enter_context(tc.tile_pool(name="xraw", bufs=BATCH))
+        stage = ctx.enter_context(tc.tile_pool(name="stage", bufs=3))
+        outp = ctx.enter_context(tc.tile_pool(name="outp", bufs=6))
+        psum = ctx.enter_context(tc.psum_pool(name="psum", bufs=4))
+
+        e_raw = const.tile([P, PACK, NODES], BF16)
+        nc.sync.dma_start(out=e_raw[:], in_=edge_w.rearrange("(j p) d -> p j d", p=P))
+        w_raw = const.tile([P, PACK, TIME], BF16)
+        nc.sync.dma_start(out=w_raw[:], in_=weight.rearrange("(p j) o -> p j o", j=PACK))
+        x_raw = []
+        for b in range(BATCH):
+            xr = xraw_pool.tile([P, PACK, NODES], BF16, name="xr", tag="xr")
+            nc.sync.dma_start(out=xr[:], in_=x[b].rearrange("(p j) s -> p j s", j=PACK))
+            x_raw.append(xr)
+            if b == 0:
+                b_raw = const.tile([P, PACK], BF16)
+                nc.sync.dma_start(out=b_raw[:], in_=bias.rearrange("(m c) -> m c", c=PACK))
+
+        ones = const.tile([P, P], BF16)
+        nc.vector.memset(ones[:], 1.0)
+        one_col = const.tile([P, 1], F32)
+        nc.vector.memset(one_col[:], 1.0)
+        junk = const.tile([P, 1], F32)
+        nc.scalar.activation(out=junk[:], in_=one_col[:], func=ACT.Sqrt)
+        ident = const.tile([P, P], F32)
+        make_identity(nc, ident[:])
+
+        xq = {}
+        xwp = {}
+        xwg = {}
+        xwq = {}
+        ops = {}
+
+        def regroup(b):
+            g = stage.tile([P, NODES, PACK], BF16, name="xg", tag="xg", align_bytes=64)
+            dst = g[:].rearrange("p (c i) t -> p c t i", i=4)
+            src = x_raw[b][:].rearrange("p t (c i) -> p c t i", i=4)
+            if b == 1:
+                nc.scalar.copy(out=dst, in_=src)
+            else:
+                nc.vector.tensor_copy(out=dst, in_=src)
+            xq[b] = [g]
+
+        def quant_x(b):
+            g = xq[b][0]
+            codes = stage.tile([P, NODES], U32, name="xc", tag="xc", align_bytes=64)
+            scales = stage.tile([P, NODES], U8, name="xs", tag="xs", align_bytes=64)
+            nc.vector.quantize_mx(
+                out=codes[:].bitcast(FP8X4), scales=scales[:],
+                in_=g[:].rearrange("p s t -> p (s t)"),
+            )
+            xq[b] = [codes, scales]
+
+        def mm1(b):
+            codes, scales = xq[b]
+            banks = {}
+            for c in (0, 2, 1, 3):
+                acc = psum.tile([P, PACK, P], F32, name="xw", tag="xw")
+                for j in range(PACK):
+                    nc.tensor.matmul_mx(
+                        out=acc[:, j, :],
+                        lhsT=codes[:, j * P:(j + 1) * P].bitcast(FP8X4),
+                        lhsT_scale=scales[:, j * P:(j + 1) * P],
+                        rhs=w_codes[:, c * P:(c + 1) * P].bitcast(FP8X4),
+                        rhs_scale=w_scales[:, c * P:(c + 1) * P],
+                        start=True, stop=True,
+                    )
+                banks[c] = acc
+            xwp[b] = banks
+
+        def evac_xw(b):
+            g = stage.tile([P, TIME, PACK], BF16, name="xwg", tag="xwg", align_bytes=64)
+            for c in (0, 2, 1, 3):
+                src = xwp[b][c][:].rearrange("p j o -> p o j")
+                dst = g[:, c * P:(c + 1) * P, :]
+                if b < 2 or c >= 2:
+                    nc.scalar.copy(out=dst, in_=src)
+                else:
+                    nc.vector.tensor_copy(out=dst, in_=src)
+            xwg[b] = g
+
+        def quant_xw(b):
+            codes = stage.tile([P, TIME], U32, name="xwc", tag="xwc", align_bytes=64)
+            scales = stage.tile([P, TIME], U8, name="xws", tag="xws", align_bytes=64)
+            nc.vector.quantize_mx(
+                out=codes[:].bitcast(FP8X4), scales=scales[:],
+                in_=xwg[b][:].rearrange("p o j -> p (o j)"),
+            )
+            xwq[b] = [codes, scales]
+
+        def mm2(b):
+            codes, scales = xwq[b]
+            banks = []
+            for c in range(PACK):
+                acc = psum.tile([P, NODES], F32, name="op", tag="op")
+                nc.tensor.matmul_mx(
+                    out=acc[:],
+                    lhsT=codes[:, c * P:(c + 1) * P].bitcast(FP8X4),
+                    lhsT_scale=scales[:, c * P:(c + 1) * P],
+                    rhs=n_codes[:].bitcast(FP8X4),
+                    rhs_scale=n_scales[:],
+                    start=True, stop=True,
+                )
+                banks.append(acc)
+            ops[b] = banks
+
+        def evac_out(b):
+            res = outp.tile([P, PACK, NODES], F32, name="res", tag="res")
+            dram = out[b].rearrange("(m c) d -> m c d", c=PACK)
+            for c in range(PACK):
+                if b >= BATCH - 3 and c % 2 == 1:
+                    nc.vector.tensor_scalar(
+                        out=res[:, c, :], in0=ops[b][c][:], scalar1=b_col[:, c:c + 1],
+                        scalar2=None, op0=ALU.add,
+                    )
+                else:
+                    nc.scalar.activation(
+                        out=res[:, c, :], in_=ops[b][c][:], func=ACT.Identity,
+                        bias=b_col[:, c:c + 1],
+                    )
+                if b == BATCH - 1 and c % 2 == 1:
+                    nc.sync.dma_start(out=dram[:, c - 1:c + 1, :], in_=res[:, c - 1:c + 1, :])
+            if b < BATCH - 1:
+                nc.sync.dma_start(out=dram, in_=res[:])
+
+        deg_ps = psum.tile([P, PACK, 32], F32, name="deg", tag="op")
+        for j in range(PACK):
+            for k in range(PACK):
+                nc.tensor.matmul(
+                    deg_ps[:, j, :], lhsT=e_raw[:, k, j * P:(j + 1) * P], rhs=ones[:, 0:32],
+                    start=(k == 0), stop=(k == PACK - 1),
+                )
+        w_grp = const.tile([P, TIME, PACK], BF16, align_bytes=64)
+        nc.vector.tensor_copy(
+            out=w_grp[:].rearrange("p (c m) j -> p c m j", c=PACK),
+            in_=w_raw[:].rearrange("p j (m c) -> p c m j", c=PACK),
+        )
+        notpos = const.tile([P, PACK], F32)
+        nc.vector.tensor_single_scalar(out=notpos[:], in_=deg_ps[:, :, 0], scalar=0.0, op=ALU.is_le)
+        safe = const.tile([P, PACK], F32)
+        nc.vector.tensor_tensor(out=safe[:], in0=deg_ps[:, :, 0], in1=notpos[:], op=ALU.max)
+        root = const.tile([P, PACK], F32)
+        nc.scalar.activation(out=root[:], in_=safe[:], func=ACT.Sqrt)
+        pos = const.tile([P, PACK], F32)
+        nc.vector.tensor_single_scalar(out=pos[:], in_=deg_ps[:, :, 0], scalar=0.0, op=ALU.is_gt)
+        rinv = const.tile([P, PACK], F32)
+        nc.vector.reciprocal(out=rinv[:], in_=root[:])
+        dinv = const.tile([P, PACK], F32)
+        nc.vector.tensor_tensor(out=dinv[:], in0=rinv[:], in1=pos[:], op=ALU.mult)
+        drow_ps = psum.tile([P, NODES], F32, name="drow", tag="op")
+        for j in range(PACK):
+            nc.tensor.matmul(
+                drow_ps[:, j * P:(j + 1) * P], lhsT=dinv[:, j:j + 1].to_broadcast([P, P]),
+                rhs=ident[:], start=True, stop=True,
+            )
+        half = const.tile([P, PACK, NODES], F32)
+        for j in range(PACK):
+            nc.scalar.activation(
+                out=half[:, j, :], in_=e_raw[:, j, :], func=ACT.Copy, scale=dinv[:, j:j + 1],
+            )
+        regroup(0)
+        w_codes = const.tile([P, TIME], U32, align_bytes=64)
+        w_scales = const.tile([P, TIME], U8, align_bytes=64)
+        nc.vector.quantize_mx(
+            out=w_codes[:].bitcast(FP8X4), scales=w_scales[:],
+            in_=w_grp[:].rearrange("p o j -> p (o j)"),
+        )
+        quant_x(0)
+        mm1(0)
+        b_col = const.tile([P, PACK], F32)
+        nc.vector.tensor_copy(out=b_col[:], in_=b_raw[:])
+        regroup(1)
+        n_grp = const.tile([P, NODES, PACK], BF16, align_bytes=64)
+        nc.vector.tensor_tensor(
+            out=n_grp[:], in0=half[:].rearrange("p j d -> p d j"),
+            in1=drow_ps[:].unsqueeze(2).to_broadcast([P, NODES, PACK]), op=ALU.mult,
+        )
+        quant_x(1)
+        n_codes = const.tile([P, NODES], U32, align_bytes=64)
+        n_scales = const.tile([P, NODES], U8, align_bytes=64)
+        nc.vector.quantize_mx(
+            out=n_codes[:].bitcast(FP8X4), scales=n_scales[:],
+            in_=n_grp[:].rearrange("p d j -> p (d j)"),
+        )
+
+        for i in range(BATCH + 1):
+            if i < BATCH:
+                evac_xw(i)
+            if i >= 1:
+                evac_out(i - 1)
+            if i + 2 < BATCH:
+                regroup(i + 2)
+            if i + 1 < BATCH:
+                mm1(i + 1)
+            if i < BATCH:
+                quant_xw(i)
+            if i + 2 < BATCH:
+                quant_x(i + 2)
+            if i < BATCH:
+                mm2(i)

@@ -18,14 +18,15 @@ BATCH = 16
 TIME = 512
 FLOPS = 2 * 2 * NODES * BATCH * TIME * TIME
 
-PIN = True
+LEAD = 2
+V_COLS = 320
+BANK_ORDER = (0, 2, 1, 3)
 
 
 def tile_graphembedding_pa_t_kernel(tc, x, edge_w, weight, bias, out):
     nc = tc.nc
     with ExitStack() as ctx:
-        if PIN:
-            ctx.enter_context(tc.manual_schedule())
+        ctx.enter_context(tc.manual_schedule())
         const = ctx.enter_context(tc.tile_pool(name="const", bufs=1))
         xraw_pool = ctx.enter_context(tc.tile_pool(name="xraw", bufs=BATCH))
         stage = ctx.enter_context(tc.tile_pool(name="stage", bufs=3))
@@ -54,36 +55,51 @@ def tile_graphembedding_pa_t_kernel(tc, x, edge_w, weight, bias, out):
         ident = const.tile([P, P], F32)
         make_identity(nc, ident[:])
 
-        xq = {}
-        xwp = {}
-        xwg = {}
-        xwq = {}
-        ops = {}
+        x_grp = {}
+        x_mx = {}
+        xw_ps = {}
+        xw_grp = {}
+        xw_mx = {}
+        out_ps = {}
 
-        def regroup(b):
-            g = stage.tile([P, NODES, PACK], BF16, name="xg", tag="xg", align_bytes=64)
-            dst = g[:].rearrange("p (c i) t -> p c t i", i=4)
-            src = x_raw[b][:].rearrange("p t (c i) -> p c t i", i=4)
-            if b == 1:
-                nc.scalar.copy(out=dst, in_=src)
-            else:
-                nc.vector.tensor_copy(out=dst, in_=src)
-            xq[b] = [g]
-
-        def quant_x(b):
-            g = xq[b][0]
-            codes = stage.tile([P, NODES], U32, name="xc", tag="xc", align_bytes=64)
-            scales = stage.tile([P, NODES], U8, name="xs", tag="xs", align_bytes=64)
+        def quantise(grouped, tag):
+            codes = stage.tile([P, 512], U32, name=tag + "c", tag=tag + "c", align_bytes=64)
+            scales = stage.tile([P, 512], U8, name=tag + "s", tag=tag + "s", align_bytes=64)
             nc.vector.quantize_mx(
                 out=codes[:].bitcast(FP8X4), scales=scales[:],
-                in_=g[:].rearrange("p s t -> p (s t)"),
+                in_=grouped[:].rearrange("p w j -> p (w j)"),
             )
-            xq[b] = [codes, scales]
+            return codes, scales
 
-        def mm1(b):
-            codes, scales = xq[b]
-            banks = {}
-            for c in (0, 2, 1, 3):
+        def regroup_x(b):
+            g = stage.tile([P, NODES, PACK], BF16, name="xg", tag="xg", align_bytes=64)
+            raw = x_raw[b]
+            if b == 1:
+                nc.scalar.copy(
+                    out=g[:].rearrange("p (c i) t -> p c t i", i=4),
+                    in_=raw[:].rearrange("p t (c i) -> p c t i", i=4),
+                )
+            else:
+                cols = NODES if b == 0 else V_COLS
+                nc.vector.tensor_copy(
+                    out=g[:, 0:cols, :].rearrange("p (c i) t -> p c t i", i=4),
+                    in_=raw[:, :, 0:cols].rearrange("p t (c i) -> p c t i", i=4),
+                )
+                if cols < NODES:
+                    nc.gpsimd.tensor_scalar(
+                        out=g[:, cols:NODES, :],
+                        in0=raw[:, :, cols:NODES].rearrange("p t s -> p s t"),
+                        scalar1=1.0, scalar2=0.0, op0=ALU.mult, op1=ALU.add,
+                    )
+            x_grp[b] = g
+
+        def quantise_x(b):
+            x_mx[b] = quantise(x_grp[b], "x")
+
+        def first_matmul(b):
+            codes, scales = x_mx[b]
+            xw_ps[b] = {}
+            for c in BANK_ORDER:
                 acc = psum.tile([P, PACK, P], F32, name="xw", tag="xw")
                 for j in range(PACK):
                     nc.tensor.matmul_mx(
@@ -94,32 +110,25 @@ def tile_graphembedding_pa_t_kernel(tc, x, edge_w, weight, bias, out):
                         rhs_scale=w_scales[:, c * P:(c + 1) * P],
                         start=True, stop=True,
                     )
-                banks[c] = acc
-            xwp[b] = banks
+                xw_ps[b][c] = acc
 
-        def evac_xw(b):
+        def evacuate_xw(b):
             g = stage.tile([P, TIME, PACK], BF16, name="xwg", tag="xwg", align_bytes=64)
-            for c in (0, 2, 1, 3):
-                src = xwp[b][c][:].rearrange("p j o -> p o j")
+            for c in BANK_ORDER:
+                src = xw_ps[b][c][:].rearrange("p j o -> p o j")
                 dst = g[:, c * P:(c + 1) * P, :]
-                if b < 2 or c >= 2:
+                if b == 0 or c >= 2:
                     nc.scalar.copy(out=dst, in_=src)
                 else:
                     nc.vector.tensor_copy(out=dst, in_=src)
-            xwg[b] = g
+            xw_grp[b] = g
 
-        def quant_xw(b):
-            codes = stage.tile([P, TIME], U32, name="xwc", tag="xwc", align_bytes=64)
-            scales = stage.tile([P, TIME], U8, name="xws", tag="xws", align_bytes=64)
-            nc.vector.quantize_mx(
-                out=codes[:].bitcast(FP8X4), scales=scales[:],
-                in_=xwg[b][:].rearrange("p o j -> p (o j)"),
-            )
-            xwq[b] = [codes, scales]
+        def quantise_xw(b):
+            xw_mx[b] = quantise(xw_grp[b], "xw")
 
-        def mm2(b):
-            codes, scales = xwq[b]
-            banks = []
+        def second_matmul(b):
+            codes, scales = xw_mx[b]
+            out_ps[b] = []
             for c in range(PACK):
                 acc = psum.tile([P, NODES], F32, name="op", tag="op")
                 nc.tensor.matmul_mx(
@@ -130,27 +139,27 @@ def tile_graphembedding_pa_t_kernel(tc, x, edge_w, weight, bias, out):
                     rhs_scale=n_scales[:],
                     start=True, stop=True,
                 )
-                banks.append(acc)
-            ops[b] = banks
+                out_ps[b].append(acc)
 
-        def evac_out(b):
+        def evacuate_out(b):
             res = outp.tile([P, PACK, NODES], F32, name="res", tag="res")
             dram = out[b].rearrange("(m c) d -> m c d", c=PACK)
+            last = b == BATCH - 1
             for c in range(PACK):
-                if b >= BATCH - 3 and c % 2 == 1:
+                if (c == 3 and b % 4 == 3) or (c % 2 == 1 and b + 1 + LEAD >= BATCH):
                     nc.vector.tensor_scalar(
-                        out=res[:, c, :], in0=ops[b][c][:], scalar1=b_col[:, c:c + 1],
+                        out=res[:, c, :], in0=out_ps[b][c][:], scalar1=b_col[:, c:c + 1],
                         scalar2=None, op0=ALU.add,
                     )
                 else:
                     nc.scalar.activation(
-                        out=res[:, c, :], in_=ops[b][c][:], func=ACT.Identity,
+                        out=res[:, c, :], in_=out_ps[b][c][:], func=ACT.Identity,
                         bias=b_col[:, c:c + 1],
                     )
-                if b == BATCH - 1 and c % 2 == 1:
+                if last:
+                    nc.sync.dma_start(out=dram[:, c, :], in_=res[:, c, :])
+                elif c % 2 == 1:
                     nc.sync.dma_start(out=dram[:, c - 1:c + 1, :], in_=res[:, c - 1:c + 1, :])
-            if b < BATCH - 1:
-                nc.sync.dma_start(out=dram, in_=res[:])
 
         deg_ps = psum.tile([P, PACK, 32], F32, name="deg", tag="op")
         for j in range(PACK):
@@ -187,43 +196,33 @@ def tile_graphembedding_pa_t_kernel(tc, x, edge_w, weight, bias, out):
             nc.scalar.activation(
                 out=half[:, j, :], in_=e_raw[:, j, :], func=ACT.Copy, scale=dinv[:, j:j + 1],
             )
-        regroup(0)
-        w_codes = const.tile([P, TIME], U32, align_bytes=64)
-        w_scales = const.tile([P, TIME], U8, align_bytes=64)
-        nc.vector.quantize_mx(
-            out=w_codes[:].bitcast(FP8X4), scales=w_scales[:],
-            in_=w_grp[:].rearrange("p o j -> p (o j)"),
-        )
-        quant_x(0)
-        mm1(0)
+        regroup_x(0)
+        w_codes, w_scales = quantise(w_grp, "w")
+        quantise_x(0)
+        first_matmul(0)
         b_col = const.tile([P, PACK], F32)
         nc.vector.tensor_copy(out=b_col[:], in_=b_raw[:])
-        regroup(1)
+        regroup_x(1)
         n_grp = const.tile([P, NODES, PACK], BF16, align_bytes=64)
         nc.vector.tensor_tensor(
             out=n_grp[:], in0=half[:].rearrange("p j d -> p d j"),
             in1=drow_ps[:].unsqueeze(2).to_broadcast([P, NODES, PACK]), op=ALU.mult,
         )
-        quant_x(1)
-        n_codes = const.tile([P, NODES], U32, align_bytes=64)
-        n_scales = const.tile([P, NODES], U8, align_bytes=64)
-        nc.vector.quantize_mx(
-            out=n_codes[:].bitcast(FP8X4), scales=n_scales[:],
-            in_=n_grp[:].rearrange("p d j -> p (d j)"),
-        )
+        quantise_x(1)
+        n_codes, n_scales = quantise(n_grp, "n")
 
         for i in range(BATCH + 1):
             if i < BATCH:
-                evac_xw(i)
+                evacuate_xw(i)
             if i >= 1:
-                evac_out(i - 1)
-            if i + 2 < BATCH:
-                regroup(i + 2)
+                evacuate_out(i - 1)
+            if i + LEAD < BATCH:
+                regroup_x(i + LEAD)
             if i + 1 < BATCH:
-                mm1(i + 1)
+                first_matmul(i + 1)
             if i < BATCH:
-                quant_xw(i)
-            if i + 2 < BATCH:
-                quant_x(i + 2)
+                quantise_xw(i)
+            if i + LEAD < BATCH:
+                quantise_x(i + LEAD)
             if i < BATCH:
-                mm2(i)
+                second_matmul(i)

@@ -19,7 +19,7 @@ TIME = 512
 FLOPS = 2 * 2 * NODES * BATCH * TIME * TIME
 
 LEAD = 2
-V_COLS = 320
+V_COLS = 352
 BANK_ORDER = (0, 2, 1, 3)
 
 
@@ -146,7 +146,7 @@ def tile_graphembedding_pa_t_kernel(tc, x, edge_w, weight, bias, out):
             dram = out[b].rearrange("(m c) d -> m c d", c=PACK)
             last = b == BATCH - 1
             for c in range(PACK):
-                if (c == 3 and b % 4 == 3) or (c % 2 == 1 and b + 1 + LEAD >= BATCH):
+                if (c == 3 and b % 3 == 2) or (c % 2 == 1 and b + 2 + LEAD >= BATCH):
                     nc.vector.tensor_scalar(
                         out=res[:, c, :], in0=out_ps[b][c][:], scalar1=b_col[:, c:c + 1],
                         scalar2=None, op0=ALU.add,
@@ -209,6 +209,7 @@ def tile_graphembedding_pa_t_kernel(tc, x, edge_w, weight, bias, out):
             in1=drow_ps[:].unsqueeze(2).to_broadcast([P, NODES, PACK]), op=ALU.mult,
         )
         quantise_x(1)
+        regroup_x(2)
         n_codes, n_scales = quantise(n_grp, "n")
 
         for i in range(BATCH + 1):
@@ -216,13 +217,12 @@ def tile_graphembedding_pa_t_kernel(tc, x, edge_w, weight, bias, out):
                 evacuate_xw(i)
             if i >= 1:
                 evacuate_out(i - 1)
-            if i + LEAD < BATCH:
-                regroup_x(i + LEAD)
+            if i + LEAD + 1 < BATCH:
+                regroup_x(i + LEAD + 1)
             if i + 1 < BATCH:
                 first_matmul(i + 1)
-            if i < BATCH:
-                quantise_xw(i)
             if i + LEAD < BATCH:
                 quantise_x(i + LEAD)
             if i < BATCH:
+                quantise_xw(i)
                 second_matmul(i)

@@ -19,7 +19,7 @@ TIME = 512
 FLOPS = 2 * 2 * NODES * BATCH * TIME * TIME
 
 LEAD = 2
-V_COLS = 352
+V_COLS = 320
 BANK_ORDER = (0, 2, 1, 3)
 
 
@@ -117,7 +117,7 @@ def tile_graphembedding_pa_t_kernel(tc, x, edge_w, weight, bias, out):
             for c in BANK_ORDER:
                 src = xw_ps[b][c][:].rearrange("p j o -> p o j")
                 dst = g[:, c * P:(c + 1) * P, :]
-                if b == 0 or c >= 2:
+                if b < 2 or c >= 2:
                     nc.scalar.copy(out=dst, in_=src)
                 else:
                     nc.vector.tensor_copy(out=dst, in_=src)
@@ -146,7 +146,7 @@ def tile_graphembedding_pa_t_kernel(tc, x, edge_w, weight, bias, out):
             dram = out[b].rearrange("(m c) d -> m c d", c=PACK)
             last = b == BATCH - 1
             for c in range(PACK):
-                if (c == 3 and b % 3 == 2) or (c % 2 == 1 and b + 2 + LEAD >= BATCH):
+                if c % 2 == 1 and b + 1 + LEAD >= BATCH:
                     nc.vector.tensor_scalar(
                         out=res[:, c, :], in0=out_ps[b][c][:], scalar1=b_col[:, c:c + 1],
                         scalar2=None, op0=ALU.add,
@@ -209,7 +209,6 @@ def tile_graphembedding_pa_t_kernel(tc, x, edge_w, weight, bias, out):
             in1=drow_ps[:].unsqueeze(2).to_broadcast([P, NODES, PACK]), op=ALU.mult,
         )
         quantise_x(1)
-        regroup_x(2)
         n_codes, n_scales = quantise(n_grp, "n")
 
         for i in range(BATCH + 1):
@@ -217,12 +216,13 @@ def tile_graphembedding_pa_t_kernel(tc, x, edge_w, weight, bias, out):
                 evacuate_xw(i)
             if i >= 1:
                 evacuate_out(i - 1)
-            if i + LEAD + 1 < BATCH:
-                regroup_x(i + LEAD + 1)
+            if i + LEAD < BATCH:
+                regroup_x(i + LEAD)
             if i + 1 < BATCH:
                 first_matmul(i + 1)
+            if i < BATCH:
+                quantise_xw(i)
             if i + LEAD < BATCH:
                 quantise_x(i + LEAD)
             if i < BATCH:
-                quantise_xw(i)
                 second_matmul(i)

@@ -20,7 +20,6 @@ FLOPS = 2 * 2 * NODES * BATCH * TIME * TIME
 
 LEAD = 2
 V_COLS = 320
-BANK_ORDER = (0, 2, 1, 3)
 
 
 def tile_graphembedding_pa_t_kernel(tc, x, edge_w, weight, bias, out):
@@ -74,23 +73,17 @@ def tile_graphembedding_pa_t_kernel(tc, x, edge_w, weight, bias, out):
         def regroup_x(b):
             g = stage.tile([P, NODES, PACK], BF16, name="xg", tag="xg", align_bytes=64)
             raw = x_raw[b]
-            if b == 1:
-                nc.scalar.copy(
-                    out=g[:].rearrange("p (c i) t -> p c t i", i=4),
-                    in_=raw[:].rearrange("p t (c i) -> p c t i", i=4),
+            cols = NODES if b == 0 else V_COLS
+            nc.vector.tensor_copy(
+                out=g[:, 0:cols, :].rearrange("p (c i) t -> p c t i", i=4),
+                in_=raw[:, :, 0:cols].rearrange("p t (c i) -> p c t i", i=4),
+            )
+            if cols < NODES:
+                nc.gpsimd.tensor_scalar(
+                    out=g[:, cols:NODES, :],
+                    in0=raw[:, :, cols:NODES].rearrange("p t s -> p s t"),
+                    scalar1=1.0, scalar2=0.0, op0=ALU.mult, op1=ALU.add,
                 )
-            else:
-                cols = NODES if b == 0 else V_COLS
-                nc.vector.tensor_copy(
-                    out=g[:, 0:cols, :].rearrange("p (c i) t -> p c t i", i=4),
-                    in_=raw[:, :, 0:cols].rearrange("p t (c i) -> p c t i", i=4),
-                )
-                if cols < NODES:
-                    nc.gpsimd.tensor_scalar(
-                        out=g[:, cols:NODES, :],
-                        in0=raw[:, :, cols:NODES].rearrange("p t s -> p s t"),
-                        scalar1=1.0, scalar2=0.0, op0=ALU.mult, op1=ALU.add,
-                    )
             x_grp[b] = g
 
         def quantise_x(b):
@@ -99,7 +92,7 @@ def tile_graphembedding_pa_t_kernel(tc, x, edge_w, weight, bias, out):
         def first_matmul(b):
             codes, scales = x_mx[b]
             xw_ps[b] = {}
-            for c in BANK_ORDER:
+            for c in range(PACK):
                 acc = psum.tile([P, PACK, P], F32, name="xw", tag="xw")
                 for j in range(PACK):
                     nc.tensor.matmul_mx(
@@ -114,10 +107,10 @@ def tile_graphembedding_pa_t_kernel(tc, x, edge_w, weight, bias, out):
 
         def evacuate_xw(b):
             g = stage.tile([P, TIME, PACK], BF16, name="xwg", tag="xwg", align_bytes=64)
-            for c in BANK_ORDER:
+            for c in range(PACK):
                 src = xw_ps[b][c][:].rearrange("p j o -> p o j")
                 dst = g[:, c * P:(c + 1) * P, :]
-                if b < 2 or c >= 2:
+                if b < 3 or c >= 1:
                     nc.scalar.copy(out=dst, in_=src)
                 else:
                     nc.vector.tensor_copy(out=dst, in_=src)
@@ -128,8 +121,8 @@ def tile_graphembedding_pa_t_kernel(tc, x, edge_w, weight, bias, out):
 
         def second_matmul(b):
             codes, scales = xw_mx[b]
-            out_ps[b] = []
-            for c in range(PACK):
+            out_ps[b] = {}
+            for c in (3, 0, 1, 2):
                 acc = psum.tile([P, NODES], F32, name="op", tag="op")
                 nc.tensor.matmul_mx(
                     out=acc[:],
@@ -139,14 +132,14 @@ def tile_graphembedding_pa_t_kernel(tc, x, edge_w, weight, bias, out):
                     rhs_scale=n_scales[:],
                     start=True, stop=True,
                 )
-                out_ps[b].append(acc)
+                out_ps[b][c] = acc
 
         def evacuate_out(b):
             res = outp.tile([P, PACK, NODES], F32, name="res", tag="res")
             dram = out[b].rearrange("(m c) d -> m c d", c=PACK)
             last = b == BATCH - 1
             for c in range(PACK):
-                if c % 2 == 1 and b + 1 + LEAD >= BATCH:
+                if c == 3 or (c == 1 and b + 1 + LEAD >= BATCH):
                     nc.vector.tensor_scalar(
                         out=res[:, c, :], in0=out_ps[b][c][:], scalar1=b_col[:, c:c + 1],
                         scalar2=None, op0=ALU.add,

@@ -20,6 +20,7 @@ FLOPS = 2 * 2 * NODES * BATCH * TIME * TIME
 
 LEAD = 2
 V_COLS = 320
+BANK_ORDER = (0, 2, 1, 3)
 
 
 def tile_graphembedding_pa_t_kernel(tc, x, edge_w, weight, bias, out):
@@ -33,7 +34,8 @@ def tile_graphembedding_pa_t_kernel(tc, x, edge_w, weight, bias, out):
         psum = ctx.enter_context(tc.psum_pool(name="psum", bufs=4))
 
         e_raw = const.tile([P, PACK, NODES], BF16)
-        nc.sync.dma_start(out=e_raw[:], in_=edge_w.rearrange("(j p) d -> p j d", p=P))
+        for k in range(PACK):
+            nc.sync.dma_start(out=e_raw[:, k, :], in_=edge_w[k * P:(k + 1) * P, :])
         w_raw = const.tile([P, PACK, TIME], BF16)
         nc.sync.dma_start(out=w_raw[:], in_=weight.rearrange("(p j) o -> p j o", j=PACK))
         x_raw = []
@@ -73,17 +75,23 @@ def tile_graphembedding_pa_t_kernel(tc, x, edge_w, weight, bias, out):
         def regroup_x(b):
             g = stage.tile([P, NODES, PACK], BF16, name="xg", tag="xg", align_bytes=64)
             raw = x_raw[b]
-            cols = NODES if b == 0 else V_COLS
-            nc.vector.tensor_copy(
-                out=g[:, 0:cols, :].rearrange("p (c i) t -> p c t i", i=4),
-                in_=raw[:, :, 0:cols].rearrange("p t (c i) -> p c t i", i=4),
-            )
-            if cols < NODES:
-                nc.gpsimd.tensor_scalar(
-                    out=g[:, cols:NODES, :],
-                    in0=raw[:, :, cols:NODES].rearrange("p t s -> p s t"),
-                    scalar1=1.0, scalar2=0.0, op0=ALU.mult, op1=ALU.add,
+            if b == 1:
+                nc.scalar.copy(
+                    out=g[:].rearrange("p (c i) t -> p c t i", i=4),
+                    in_=raw[:].rearrange("p t (c i) -> p c t i", i=4),
                 )
+            else:
+                cols = NODES if b == 0 else V_COLS
+                nc.vector.tensor_copy(
+                    out=g[:, 0:cols, :].rearrange("p (c i) t -> p c t i", i=4),
+                    in_=raw[:, :, 0:cols].rearrange("p t (c i) -> p c t i", i=4),
+                )
+                if cols < NODES:
+                    nc.gpsimd.tensor_scalar(
+                        out=g[:, cols:NODES, :],
+                        in0=raw[:, :, cols:NODES].rearrange("p t s -> p s t"),
+                        scalar1=1.0, scalar2=0.0, op0=ALU.mult, op1=ALU.add,
+                    )
             x_grp[b] = g
 
         def quantise_x(b):
@@ -92,7 +100,7 @@ def tile_graphembedding_pa_t_kernel(tc, x, edge_w, weight, bias, out):
         def first_matmul(b):
             codes, scales = x_mx[b]
             xw_ps[b] = {}
-            for c in range(PACK):
+            for c in BANK_ORDER:
                 acc = psum.tile([P, PACK, P], F32, name="xw", tag="xw")
                 for j in range(PACK):
                     nc.tensor.matmul_mx(
@@ -107,10 +115,10 @@ def tile_graphembedding_pa_t_kernel(tc, x, edge_w, weight, bias, out):
 
         def evacuate_xw(b):
             g = stage.tile([P, TIME, PACK], BF16, name="xwg", tag="xwg", align_bytes=64)
-            for c in range(PACK):
+            for c in BANK_ORDER:
                 src = xw_ps[b][c][:].rearrange("p j o -> p o j")
                 dst = g[:, c * P:(c + 1) * P, :]
-                if b < 3 or c >= 1:
+                if b < 2 or c >= 2:
                     nc.scalar.copy(out=dst, in_=src)
                 else:
                     nc.vector.tensor_copy(out=dst, in_=src)
@@ -121,8 +129,8 @@ def tile_graphembedding_pa_t_kernel(tc, x, edge_w, weight, bias, out):
 
         def second_matmul(b):
             codes, scales = xw_mx[b]
-            out_ps[b] = {}
-            for c in (3, 0, 1, 2):
+            out_ps[b] = []
+            for c in range(PACK):
                 acc = psum.tile([P, NODES], F32, name="op", tag="op")
                 nc.tensor.matmul_mx(
                     out=acc[:],
@@ -132,14 +140,14 @@ def tile_graphembedding_pa_t_kernel(tc, x, edge_w, weight, bias, out):
                     rhs_scale=n_scales[:],
                     start=True, stop=True,
                 )
-                out_ps[b][c] = acc
+                out_ps[b].append(acc)
 
         def evacuate_out(b):
             res = outp.tile([P, PACK, NODES], F32, name="res", tag="res")
             dram = out[b].rearrange("(m c) d -> m c d", c=PACK)
             last = b == BATCH - 1
             for c in range(PACK):
-                if c == 3 or (c == 1 and b + 1 + LEAD >= BATCH):
+                if c % 2 == 1 and b + 1 + LEAD >= BATCH:
                     nc.vector.tensor_scalar(
                         out=res[:, c, :], in0=out_ps[b][c][:], scalar1=b_col[:, c:c + 1],
                         scalar2=None, op0=ALU.add,
@@ -154,30 +162,32 @@ def tile_graphembedding_pa_t_kernel(tc, x, edge_w, weight, bias, out):
                 elif c % 2 == 1:
                     nc.sync.dma_start(out=dram[:, c - 1:c + 1, :], in_=res[:, c - 1:c + 1, :])
 
-        deg_ps = psum.tile([P, PACK, 32], F32, name="deg", tag="op")
-        for j in range(PACK):
-            for k in range(PACK):
+        deg_ps = psum.tile([P, PACK, PACK, 32], F32, name="deg", tag="op")
+        for k in range(PACK):
+            for j in range(PACK):
                 nc.tensor.matmul(
-                    deg_ps[:, j, :], lhsT=e_raw[:, k, j * P:(j + 1) * P], rhs=ones[:, 0:32],
-                    start=(k == 0), stop=(k == PACK - 1),
+                    deg_ps[:, j, k, :], lhsT=e_raw[:, k, j * P:(j + 1) * P], rhs=ones[:, 0:32],
+                    start=True, stop=True,
                 )
+        deg = const.tile([P, PACK], F32)
+        nc.vector.tensor_reduce(out=deg[:], in_=deg_ps[:, :, :, 0], axis=mybir.AxisListType.X, op=ALU.add)
+        notpos = const.tile([P, PACK], F32)
+        nc.vector.tensor_single_scalar(out=notpos[:], in_=deg[:], scalar=0.0, op=ALU.is_le)
+        safe = const.tile([P, PACK], F32)
+        nc.vector.tensor_tensor(out=safe[:], in0=deg[:], in1=notpos[:], op=ALU.max)
+        root = const.tile([P, PACK], F32)
+        nc.scalar.activation(out=root[:], in_=safe[:], func=ACT.Sqrt)
+        pos = const.tile([P, PACK], F32)
+        nc.vector.tensor_single_scalar(out=pos[:], in_=deg[:], scalar=0.0, op=ALU.is_gt)
+        rinv = const.tile([P, PACK], F32)
+        nc.vector.reciprocal(out=rinv[:], in_=root[:])
+        dinv = const.tile([P, PACK], F32)
+        nc.vector.tensor_tensor(out=dinv[:], in0=rinv[:], in1=pos[:], op=ALU.mult)
         w_grp = const.tile([P, TIME, PACK], BF16, align_bytes=64)
         nc.vector.tensor_copy(
             out=w_grp[:].rearrange("p (c m) j -> p c m j", c=PACK),
             in_=w_raw[:].rearrange("p j (m c) -> p c m j", c=PACK),
         )
-        notpos = const.tile([P, PACK], F32)
-        nc.vector.tensor_single_scalar(out=notpos[:], in_=deg_ps[:, :, 0], scalar=0.0, op=ALU.is_le)
-        safe = const.tile([P, PACK], F32)
-        nc.vector.tensor_tensor(out=safe[:], in0=deg_ps[:, :, 0], in1=notpos[:], op=ALU.max)
-        root = const.tile([P, PACK], F32)
-        nc.scalar.activation(out=root[:], in_=safe[:], func=ACT.Sqrt)
-        pos = const.tile([P, PACK], F32)
-        nc.vector.tensor_single_scalar(out=pos[:], in_=deg_ps[:, :, 0], scalar=0.0, op=ALU.is_gt)
-        rinv = const.tile([P, PACK], F32)
-        nc.vector.reciprocal(out=rinv[:], in_=root[:])
-        dinv = const.tile([P, PACK], F32)
-        nc.vector.tensor_tensor(out=dinv[:], in0=rinv[:], in1=pos[:], op=ALU.mult)
         drow_ps = psum.tile([P, NODES], F32, name="drow", tag="op")
         for j in range(PACK):
             nc.tensor.matmul(

@@ -20,7 +20,8 @@ FLOPS = 2 * 2 * NODES * BATCH * TIME * TIME
 
 LEAD = 2
 V_COLS = 320
-BANK_ORDER = (0, 2, 1, 3)
+START_UP = 2
+ONES_COLS = 32
 
 
 def tile_graphembedding_pa_t_kernel(tc, x, edge_w, weight, bias, out):
@@ -37,11 +38,11 @@ def tile_graphembedding_pa_t_kernel(tc, x, edge_w, weight, bias, out):
         for k in range(PACK):
             nc.sync.dma_start(out=e_raw[:, k, :], in_=edge_w[k * P:(k + 1) * P, :])
         w_raw = const.tile([P, PACK, TIME], BF16)
-        nc.sync.dma_start(out=w_raw[:], in_=weight.rearrange("(p j) o -> p j o", j=PACK))
+        nc.sync.dma_start(out=w_raw[:], in_=weight.rearrange("(p i) o -> p i o", i=PACK))
         x_raw = []
         for b in range(BATCH):
             xr = xraw_pool.tile([P, PACK, NODES], BF16, name="xr", tag="xr")
-            nc.sync.dma_start(out=xr[:], in_=x[b].rearrange("(p j) s -> p j s", j=PACK))
+            nc.sync.dma_start(out=xr[:], in_=x[b].rearrange("(p i) s -> p i s", i=PACK))
             x_raw.append(xr)
             if b == 0:
                 b_raw = const.tile([P, PACK], BF16)
@@ -51,8 +52,8 @@ def tile_graphembedding_pa_t_kernel(tc, x, edge_w, weight, bias, out):
         nc.vector.memset(ones[:], 1.0)
         one_col = const.tile([P, 1], F32)
         nc.vector.memset(one_col[:], 1.0)
-        junk = const.tile([P, 1], F32)
-        nc.scalar.activation(out=junk[:], in_=one_col[:], func=ACT.Sqrt)
+        unused_root = const.tile([P, 1], F32)
+        nc.scalar.activation(out=unused_root[:], in_=one_col[:], func=ACT.Sqrt)
         ident = const.tile([P, P], F32)
         make_identity(nc, ident[:])
 
@@ -63,80 +64,83 @@ def tile_graphembedding_pa_t_kernel(tc, x, edge_w, weight, bias, out):
         xw_mx = {}
         out_ps = {}
 
-        def quantise(grouped, tag):
-            codes = stage.tile([P, 512], U32, name=tag + "c", tag=tag + "c", align_bytes=64)
-            scales = stage.tile([P, 512], U8, name=tag + "s", tag=tag + "s", align_bytes=64)
+        def quantise(pool, grouped, tag):
+            words = pool.tile([P, 512], U32, name=tag + "w", tag=tag + "w", align_bytes=64)
+            scales = pool.tile([P, 512], U8, name=tag + "s", tag=tag + "s", align_bytes=64)
             nc.vector.quantize_mx(
-                out=codes[:].bitcast(FP8X4), scales=scales[:],
-                in_=grouped[:].rearrange("p w j -> p (w j)"),
+                out=words[:].bitcast(FP8X4), scales=scales[:],
+                in_=grouped[:].rearrange("p w i -> p (w i)"),
             )
-            return codes, scales
+            return words, scales
+
+        def by_fours(grouped, raw, lo, hi):
+            return (
+                grouped[:, lo:hi, :].rearrange("p (g f) i -> p g i f", f=4),
+                raw[:, :, lo:hi].rearrange("p i (g f) -> p g i f", f=4),
+            )
 
         def regroup_x(b):
             g = stage.tile([P, NODES, PACK], BF16, name="xg", tag="xg", align_bytes=64)
             raw = x_raw[b]
-            if b == 1:
-                nc.scalar.copy(
-                    out=g[:].rearrange("p (c i) t -> p c t i", i=4),
-                    in_=raw[:].rearrange("p t (c i) -> p c t i", i=4),
-                )
+            if b == 0:
+                dst, src = by_fours(g, raw, 0, NODES)
+                nc.vector.tensor_copy(out=dst, in_=src)
+            elif b < START_UP:
+                dst, src = by_fours(g, raw, 0, NODES)
+                nc.scalar.copy(out=dst, in_=src)
             else:
-                cols = NODES if b == 0 else V_COLS
-                nc.vector.tensor_copy(
-                    out=g[:, 0:cols, :].rearrange("p (c i) t -> p c t i", i=4),
-                    in_=raw[:, :, 0:cols].rearrange("p t (c i) -> p c t i", i=4),
+                dst, src = by_fours(g, raw, 0, V_COLS)
+                nc.vector.tensor_copy(out=dst, in_=src)
+                nc.gpsimd.tensor_scalar(
+                    out=g[:, V_COLS:NODES, :],
+                    in0=raw[:, :, V_COLS:NODES].rearrange("p i s -> p s i"),
+                    scalar1=1.0, scalar2=0.0, op0=ALU.mult, op1=ALU.add,
                 )
-                if cols < NODES:
-                    nc.gpsimd.tensor_scalar(
-                        out=g[:, cols:NODES, :],
-                        in0=raw[:, :, cols:NODES].rearrange("p t s -> p s t"),
-                        scalar1=1.0, scalar2=0.0, op0=ALU.mult, op1=ALU.add,
-                    )
             x_grp[b] = g
 
         def quantise_x(b):
-            x_mx[b] = quantise(x_grp[b], "x")
+            x_mx[b] = quantise(stage, x_grp[b], "x")
 
         def first_matmul(b):
-            codes, scales = x_mx[b]
-            xw_ps[b] = {}
-            for c in BANK_ORDER:
-                acc = psum.tile([P, PACK, P], F32, name="xw", tag="xw")
+            words, scales = x_mx[b]
+            xw_ps[b] = []
+            for c in range(PACK):
+                acc = psum.tile([P, PACK, P], F32, name="xw_bank", tag="xw_bank")
                 for j in range(PACK):
                     nc.tensor.matmul_mx(
                         out=acc[:, j, :],
-                        lhsT=codes[:, j * P:(j + 1) * P].bitcast(FP8X4),
+                        lhsT=words[:, j * P:(j + 1) * P].bitcast(FP8X4),
                         lhsT_scale=scales[:, j * P:(j + 1) * P],
-                        rhs=w_codes[:, c * P:(c + 1) * P].bitcast(FP8X4),
+                        rhs=w_words[:, c * P:(c + 1) * P].bitcast(FP8X4),
                         rhs_scale=w_scales[:, c * P:(c + 1) * P],
                         start=True, stop=True,
                     )
-                xw_ps[b][c] = acc
+                xw_ps[b].append(acc)
 
         def evacuate_xw(b):
             g = stage.tile([P, TIME, PACK], BF16, name="xwg", tag="xwg", align_bytes=64)
-            for c in BANK_ORDER:
-                src = xw_ps[b][c][:].rearrange("p j o -> p o j")
+            for c in range(PACK):
+                src = xw_ps[b][c][:].rearrange("p j m -> p m j")
                 dst = g[:, c * P:(c + 1) * P, :]
-                if b < 2 or c >= 2:
-                    nc.scalar.copy(out=dst, in_=src)
-                else:
+                if c % 2 == 0 and b >= START_UP:
                     nc.vector.tensor_copy(out=dst, in_=src)
+                else:
+                    nc.scalar.copy(out=dst, in_=src)
             xw_grp[b] = g
 
         def quantise_xw(b):
-            xw_mx[b] = quantise(xw_grp[b], "xw")
+            xw_mx[b] = quantise(stage, xw_grp[b], "y")
 
         def second_matmul(b):
-            codes, scales = xw_mx[b]
+            words, scales = xw_mx[b]
             out_ps[b] = []
             for c in range(PACK):
-                acc = psum.tile([P, NODES], F32, name="op", tag="op")
+                acc = psum.tile([P, NODES], F32, name="out_bank", tag="out_bank")
                 nc.tensor.matmul_mx(
                     out=acc[:],
-                    lhsT=codes[:, c * P:(c + 1) * P].bitcast(FP8X4),
+                    lhsT=words[:, c * P:(c + 1) * P].bitcast(FP8X4),
                     lhsT_scale=scales[:, c * P:(c + 1) * P],
-                    rhs=n_codes[:].bitcast(FP8X4),
+                    rhs=n_words[:].bitcast(FP8X4),
                     rhs_scale=n_scales[:],
                     start=True, stop=True,
                 )
@@ -145,9 +149,9 @@ def tile_graphembedding_pa_t_kernel(tc, x, edge_w, weight, bias, out):
         def evacuate_out(b):
             res = outp.tile([P, PACK, NODES], F32, name="res", tag="res")
             dram = out[b].rearrange("(m c) d -> m c d", c=PACK)
-            last = b == BATCH - 1
+            vector_helps = b + 1 + LEAD >= BATCH
             for c in range(PACK):
-                if c % 2 == 1 and b + 1 + LEAD >= BATCH:
+                if c % 2 == 0 and vector_helps:
                     nc.vector.tensor_scalar(
                         out=res[:, c, :], in0=out_ps[b][c][:], scalar1=b_col[:, c:c + 1],
                         scalar2=None, op0=ALU.add,
@@ -157,50 +161,52 @@ def tile_graphembedding_pa_t_kernel(tc, x, edge_w, weight, bias, out):
                         out=res[:, c, :], in_=out_ps[b][c][:], func=ACT.Identity,
                         bias=b_col[:, c:c + 1],
                     )
-                if last:
+                if b == BATCH - 1:
                     nc.sync.dma_start(out=dram[:, c, :], in_=res[:, c, :])
                 elif c % 2 == 1:
                     nc.sync.dma_start(out=dram[:, c - 1:c + 1, :], in_=res[:, c - 1:c + 1, :])
 
-        deg_ps = psum.tile([P, PACK, PACK, 32], F32, name="deg", tag="op")
+        deg_ps = psum.tile([P, PACK, PACK, ONES_COLS], F32, name="deg", tag="out_bank")
         for k in range(PACK):
             for j in range(PACK):
                 nc.tensor.matmul(
-                    deg_ps[:, j, k, :], lhsT=e_raw[:, k, j * P:(j + 1) * P], rhs=ones[:, 0:32],
-                    start=True, stop=True,
+                    deg_ps[:, j, k, :], lhsT=e_raw[:, k, j * P:(j + 1) * P],
+                    rhs=ones[:, 0:ONES_COLS], start=True, stop=True,
                 )
         deg = const.tile([P, PACK], F32)
-        nc.vector.tensor_reduce(out=deg[:], in_=deg_ps[:, :, :, 0], axis=mybir.AxisListType.X, op=ALU.add)
-        notpos = const.tile([P, PACK], F32)
-        nc.vector.tensor_single_scalar(out=notpos[:], in_=deg[:], scalar=0.0, op=ALU.is_le)
+        nc.vector.tensor_reduce(
+            out=deg[:], in_=deg_ps[:, :, :, 0], axis=mybir.AxisListType.X, op=ALU.add,
+        )
         safe = const.tile([P, PACK], F32)
-        nc.vector.tensor_tensor(out=safe[:], in0=deg[:], in1=notpos[:], op=ALU.max)
+        nc.vector.scalar_tensor_tensor(
+            out=safe[:], in0=deg[:], scalar=0.0, in1=deg[:], op0=ALU.is_le, op1=ALU.max,
+        )
         root = const.tile([P, PACK], F32)
         nc.scalar.activation(out=root[:], in_=safe[:], func=ACT.Sqrt)
-        pos = const.tile([P, PACK], F32)
-        nc.vector.tensor_single_scalar(out=pos[:], in_=deg[:], scalar=0.0, op=ALU.is_gt)
         rinv = const.tile([P, PACK], F32)
         nc.vector.reciprocal(out=rinv[:], in_=root[:])
         dinv = const.tile([P, PACK], F32)
-        nc.vector.tensor_tensor(out=dinv[:], in0=rinv[:], in1=pos[:], op=ALU.mult)
+        nc.vector.scalar_tensor_tensor(
+            out=dinv[:], in0=deg[:], scalar=0.0, in1=rinv[:], op0=ALU.is_gt, op1=ALU.mult,
+        )
         w_grp = const.tile([P, TIME, PACK], BF16, align_bytes=64)
         nc.vector.tensor_copy(
-            out=w_grp[:].rearrange("p (c m) j -> p c m j", c=PACK),
-            in_=w_raw[:].rearrange("p j (m c) -> p c m j", c=PACK),
+            out=w_grp[:].rearrange("p (c m) i -> p c m i", c=PACK),
+            in_=w_raw[:].rearrange("p i (m c) -> p c m i", c=PACK),
         )
-        drow_ps = psum.tile([P, NODES], F32, name="drow", tag="op")
+        drow_ps = psum.tile([P, NODES], F32, name="drow", tag="out_bank")
         for j in range(PACK):
             nc.tensor.matmul(
                 drow_ps[:, j * P:(j + 1) * P], lhsT=dinv[:, j:j + 1].to_broadcast([P, P]),
                 rhs=ident[:], start=True, stop=True,
             )
-        half = const.tile([P, PACK, NODES], F32)
+        row_scaled = const.tile([P, PACK, NODES], F32)
         for j in range(PACK):
             nc.scalar.activation(
-                out=half[:, j, :], in_=e_raw[:, j, :], func=ACT.Copy, scale=dinv[:, j:j + 1],
+                out=row_scaled[:, j, :], in_=e_raw[:, j, :], func=ACT.Copy, scale=dinv[:, j:j + 1],
             )
         regroup_x(0)
-        w_codes, w_scales = quantise(w_grp, "w")
+        w_words, w_scales = quantise(const, w_grp, "w")
         quantise_x(0)
         first_matmul(0)
         b_col = const.tile([P, PACK], F32)
@@ -208,11 +214,11 @@ def tile_graphembedding_pa_t_kernel(tc, x, edge_w, weight, bias, out):
         regroup_x(1)
         n_grp = const.tile([P, NODES, PACK], BF16, align_bytes=64)
         nc.vector.tensor_tensor(
-            out=n_grp[:], in0=half[:].rearrange("p j d -> p d j"),
+            out=n_grp[:], in0=row_scaled[:].rearrange("p j d -> p d j"),
             in1=drow_ps[:].unsqueeze(2).to_broadcast([P, NODES, PACK]), op=ALU.mult,
         )
         quantise_x(1)
-        n_codes, n_scales = quantise(n_grp, "n")
+        n_words, n_scales = quantise(const, n_grp, "n")
 
         for i in range(BATCH + 1):
             if i < BATCH:

from contextlib import ExitStack

import concourse.mybir as mybir
from concourse.masks import make_identity

F32 = mybir.dt.float32
BF16 = mybir.dt.bfloat16
U32 = mybir.dt.uint32
U8 = mybir.dt.uint8
FP8X4 = mybir.dt.float8_e4m3fn_x4
ALU = mybir.AluOpType
ACT = mybir.ActivationFunctionType

P = 128
PACK = 4
NODES = 512
BATCH = 16
TIME = 512
FLOPS = 2 * 2 * NODES * BATCH * TIME * TIME

LEAD = 2
V_COLS = 320
START_UP = 2
ONES_COLS = 32


def tile_graphembedding_pa_t_kernel(tc, x, edge_w, weight, bias, out):
    nc = tc.nc
    with ExitStack() as ctx:
        ctx.enter_context(tc.manual_schedule())
        const = ctx.enter_context(tc.tile_pool(name="const", bufs=1))
        xraw_pool = ctx.enter_context(tc.tile_pool(name="xraw", bufs=BATCH))
        stage = ctx.enter_context(tc.tile_pool(name="stage", bufs=3))
        outp = ctx.enter_context(tc.tile_pool(name="outp", bufs=6))
        psum = ctx.enter_context(tc.psum_pool(name="psum", bufs=4))

        e_raw = const.tile([P, PACK, NODES], BF16)
        for k in range(PACK):
            nc.sync.dma_start(out=e_raw[:, k, :], in_=edge_w[k * P:(k + 1) * P, :])
        w_raw = const.tile([P, PACK, TIME], BF16)
        nc.sync.dma_start(out=w_raw[:], in_=weight.rearrange("(p i) o -> p i o", i=PACK))
        x_raw = []
        for b in range(BATCH):
            xr = xraw_pool.tile([P, PACK, NODES], BF16, name="xr", tag="xr")
            nc.sync.dma_start(out=xr[:], in_=x[b].rearrange("(p i) s -> p i s", i=PACK))
            x_raw.append(xr)
            if b == 0:
                b_raw = const.tile([P, PACK], BF16)
                nc.sync.dma_start(out=b_raw[:], in_=bias.rearrange("(m c) -> m c", c=PACK))

        ones = const.tile([P, P], BF16)
        nc.vector.memset(ones[:], 1.0)
        one_col = const.tile([P, 1], F32)
        nc.vector.memset(one_col[:], 1.0)
        unused_root = const.tile([P, 1], F32)
        nc.scalar.activation(out=unused_root[:], in_=one_col[:], func=ACT.Sqrt)
        ident = const.tile([P, P], F32)
        make_identity(nc, ident[:])

        x_grp = {}
        x_mx = {}
        xw_ps = {}
        xw_grp = {}
        xw_mx = {}
        out_ps = {}

        def quantise(pool, grouped, tag):
            words = pool.tile([P, 512], U32, name=tag + "w", tag=tag + "w", align_bytes=64)
            scales = pool.tile([P, 512], U8, name=tag + "s", tag=tag + "s", align_bytes=64)
            nc.vector.quantize_mx(
                out=words[:].bitcast(FP8X4), scales=scales[:],
                in_=grouped[:].rearrange("p w i -> p (w i)"),
            )
            return words, scales

        def by_fours(grouped, raw, lo, hi):
            return (
                grouped[:, lo:hi, :].rearrange("p (g f) i -> p g i f", f=4),
                raw[:, :, lo:hi].rearrange("p i (g f) -> p g i f", f=4),
            )

        def regroup_x(b):
            g = stage.tile([P, NODES, PACK], BF16, name="xg", tag="xg", align_bytes=64)
            raw = x_raw[b]
            if b == 0:
                dst, src = by_fours(g, raw, 0, NODES)
                nc.vector.tensor_copy(out=dst, in_=src)
            elif b < START_UP:
                dst, src = by_fours(g, raw, 0, NODES)
                nc.scalar.copy(out=dst, in_=src)
            else:
                dst, src = by_fours(g, raw, 0, V_COLS)
                nc.vector.tensor_copy(out=dst, in_=src)
                nc.gpsimd.tensor_scalar(
                    out=g[:, V_COLS:NODES, :],
                    in0=raw[:, :, V_COLS:NODES].rearrange("p i s -> p s i"),
                    scalar1=1.0, scalar2=0.0, op0=ALU.mult, op1=ALU.add,
                )
            x_grp[b] = g

        def quantise_x(b):
            x_mx[b] = quantise(stage, x_grp[b], "x")

        def first_matmul(b):
            words, scales = x_mx[b]
            xw_ps[b] = []
            for c in range(PACK):
                acc = psum.tile([P, PACK, P], F32, name="xw_bank", tag="xw_bank")
                for j in range(PACK):
                    nc.tensor.matmul_mx(
                        out=acc[:, j, :],
                        lhsT=words[:, j * P:(j + 1) * P].bitcast(FP8X4),
                        lhsT_scale=scales[:, j * P:(j + 1) * P],
                        rhs=w_words[:, c * P:(c + 1) * P].bitcast(FP8X4),
                        rhs_scale=w_scales[:, c * P:(c + 1) * P],
                        start=True, stop=True,
                    )
                xw_ps[b].append(acc)

        def evacuate_xw(b):
            g = stage.tile([P, TIME, PACK], BF16, name="xwg", tag="xwg", align_bytes=64)
            for c in range(PACK):
                src = xw_ps[b][c][:].rearrange("p j m -> p m j")
                dst = g[:, c * P:(c + 1) * P, :]
                if c % 2 == 0 and b >= START_UP:
                    nc.vector.tensor_copy(out=dst, in_=src)
                else:
                    nc.scalar.copy(out=dst, in_=src)
            xw_grp[b] = g

        def quantise_xw(b):
            xw_mx[b] = quantise(stage, xw_grp[b], "y")

        def second_matmul(b):
            words, scales = xw_mx[b]
            out_ps[b] = []
            for c in range(PACK):
                acc = psum.tile([P, NODES], F32, name="out_bank", tag="out_bank")
                nc.tensor.matmul_mx(
                    out=acc[:],
                    lhsT=words[:, c * P:(c + 1) * P].bitcast(FP8X4),
                    lhsT_scale=scales[:, c * P:(c + 1) * P],
                    rhs=n_words[:].bitcast(FP8X4),
                    rhs_scale=n_scales[:],
                    start=True, stop=True,
                )
                out_ps[b].append(acc)

        def evacuate_out(b):
            res = outp.tile([P, PACK, NODES], F32, name="res", tag="res")
            dram = out[b].rearrange("(m c) d -> m c d", c=PACK)
            vector_helps = b + 1 + LEAD >= BATCH
            for c in range(PACK):
                if c % 2 == 0 and vector_helps:
                    nc.vector.tensor_scalar(
                        out=res[:, c, :], in0=out_ps[b][c][:], scalar1=b_col[:, c:c + 1],
                        scalar2=None, op0=ALU.add,
                    )
                else:
                    nc.scalar.activation(
                        out=res[:, c, :], in_=out_ps[b][c][:], func=ACT.Identity,
                        bias=b_col[:, c:c + 1],
                    )
                if b == BATCH - 1:
                    nc.sync.dma_start(out=dram[:, c, :], in_=res[:, c, :])
                elif c % 2 == 1:
                    nc.sync.dma_start(out=dram[:, c - 1:c + 1, :], in_=res[:, c - 1:c + 1, :])

        deg_ps = psum.tile([P, PACK, PACK, ONES_COLS], F32, name="deg", tag="out_bank")
        for k in range(PACK):
            for j in range(PACK):
                nc.tensor.matmul(
                    deg_ps[:, j, k, :], lhsT=e_raw[:, k, j * P:(j + 1) * P],
                    rhs=ones[:, 0:ONES_COLS], start=True, stop=True,
                )
        deg = const.tile([P, PACK], F32)
        nc.vector.tensor_reduce(
            out=deg[:], in_=deg_ps[:, :, :, 0], axis=mybir.AxisListType.X, op=ALU.add,
        )
        safe = const.tile([P, PACK], F32)
        nc.vector.scalar_tensor_tensor(
            out=safe[:], in0=deg[:], scalar=0.0, in1=deg[:], op0=ALU.is_le, op1=ALU.max,
        )
        root = const.tile([P, PACK], F32)
        nc.scalar.activation(out=root[:], in_=safe[:], func=ACT.Sqrt)
        rinv = const.tile([P, PACK], F32)
        nc.vector.reciprocal(out=rinv[:], in_=root[:])
        dinv = const.tile([P, PACK], F32)
        nc.vector.scalar_tensor_tensor(
            out=dinv[:], in0=deg[:], scalar=0.0, in1=rinv[:], op0=ALU.is_gt, op1=ALU.mult,
        )
        w_grp = const.tile([P, TIME, PACK], BF16, align_bytes=64)
        nc.vector.tensor_copy(
            out=w_grp[:].rearrange("p (c m) i -> p c m i", c=PACK),
            in_=w_raw[:].rearrange("p i (m c) -> p c m i", c=PACK),
        )
        drow_ps = psum.tile([P, NODES], F32, name="drow", tag="out_bank")
        for j in range(PACK):
            nc.tensor.matmul(
                drow_ps[:, j * P:(j + 1) * P], lhsT=dinv[:, j:j + 1].to_broadcast([P, P]),
                rhs=ident[:], start=True, stop=True,
            )
        row_scaled = const.tile([P, PACK, NODES], F32)
        for j in range(PACK):
            nc.scalar.activation(
                out=row_scaled[:, j, :], in_=e_raw[:, j, :], func=ACT.Copy, scale=dinv[:, j:j + 1],
            )
        regroup_x(0)
        w_words, w_scales = quantise(const, w_grp, "w")
        quantise_x(0)
        first_matmul(0)
        b_col = const.tile([P, PACK], F32)
        nc.vector.tensor_copy(out=b_col[:], in_=b_raw[:])
        regroup_x(1)
        n_grp = const.tile([P, NODES, PACK], BF16, align_bytes=64)
        nc.vector.tensor_tensor(
            out=n_grp[:], in0=row_scaled[:].rearrange("p j d -> p d j"),
            in1=drow_ps[:].unsqueeze(2).to_broadcast([P, NODES, PACK]), op=ALU.mult,
        )
        quantise_x(1)
        n_words, n_scales = quantise(const, n_grp, "n")

        for i in range(BATCH + 1):
            if i < BATCH:
                evacuate_xw(i)
            if i >= 1:
                evacuate_out(i - 1)
            if i + LEAD < BATCH:
                regroup_x(i + LEAD)
            if i + 1 < BATCH:
                first_matmul(i + 1)
            if i < BATCH:
                quantise_xw(i)
            if i + LEAD < BATCH:
                quantise_x(i + LEAD)
            if i < BATCH:
                second_matmul(i)
